import numpy as np
import ml_dtypes


def mxq(x, axis, fmt="e4m3"):
    dtype, down = {"e4m3": (ml_dtypes.float8_e4m3fn, 7), "e5m2": (ml_dtypes.float8_e5m2, 14)}[fmt]
    v = np.moveaxis(np.asarray(x, np.float32).astype(ml_dtypes.bfloat16).astype(np.float64), axis, -1)
    blocks = v.reshape(v.shape[:-1] + (-1, 32))
    amax = np.abs(blocks).max(-1, keepdims=True)
    byte = np.maximum(np.where(amax > 0, np.frexp(amax)[1] - 1 + 127, 0) - down, 1)
    scale = np.exp2(byte - 127.0)
    codes = (blocks / scale).astype(np.float32).astype(dtype).astype(np.float64)
    return np.moveaxis((codes * scale).reshape(v.shape), -1, axis)


WIDE = False


def mx_kscale(k):
    if not WIDE:
        return np.ones(k)
    levels = np.array([10, -10, 5, -5, 0])
    if k % 512:
        return np.exp2(np.random.permutation(np.resize(levels, k // 32))).repeat(32)
    a = np.empty((k // 512, 16))
    for p in range(k // 512):
        a[p, :8] = np.random.permutation(np.resize(levels, 8))
        for g in range(8):
            far = levels[np.abs(levels - a[p, g]) >= 10]
            a[p, g + 8] = far[np.random.randint(len(far))]
    return np.exp2(a.ravel()).repeat(32)


BF16 = ml_dtypes.bfloat16


def bf(x):
    return np.asarray(x, np.float32).astype(BF16)


def f64(x):
    return np.asarray(x).astype(np.float64)


B, I, H = 512, 1024, 1024
FORGET_GATE_BIAS = -1.0
EPS = 1e-5


def sigmoid(v):
    return 1.0 / (1.0 + np.exp(-v))


def layer_norm_1d(x, weight, bias):
    mean = np.mean(x, axis=1, keepdims=True)
    std = np.std(x, axis=1, keepdims=True, ddof=1)
    return (x - mean) / (std + EPS) * weight + bias


def setup_inputs():
    s, t = mx_kscale(I), mx_kscale(H)
    return {
        "inputs": bf(np.random.standard_normal((B, I)) * s),
        "hx": bf(np.random.standard_normal((B, H)) * t),
        "cx": bf(np.random.standard_normal((B, H))),
        "w_i2h": bf(np.random.standard_normal((4 * H, I)) / np.sqrt(I) / s),
        "b_i2h": bf(np.random.standard_normal(4 * H) * 0.3),
        "w_h2h": bf(np.random.standard_normal((4 * H, H)) / np.sqrt(H) / t),
        "b_h2h": bf(np.random.standard_normal(4 * H) * 0.3),
        "ln_i2h_w": bf(1.0 + 0.2 * np.random.standard_normal((1, 4 * H))),
        "ln_i2h_b": bf(0.2 * np.random.standard_normal((1, 4 * H))),
        "ln_h2h_w": bf(1.0 + 0.2 * np.random.standard_normal((1, 4 * H))),
        "ln_h2h_b": bf(0.2 * np.random.standard_normal((1, 4 * H))),
        "ln_h2o_w": bf(1.0 + 0.2 * np.random.standard_normal((1, H))),
        "ln_h2o_b": bf(0.2 * np.random.standard_normal((1, H))),
    }


def reference(inputs, hx, cx, w_i2h, b_i2h, w_h2h, b_h2h,
              ln_i2h_w, ln_i2h_b, ln_h2h_w, ln_h2h_b, ln_h2o_w, ln_h2o_b):
    i2h = (mxq(f64(inputs), 1, "e4m3") @ mxq(f64(w_i2h), 1, "e4m3").T) + f64(b_i2h)
    h2h = (mxq(f64(hx), 1, "e4m3") @ mxq(f64(w_h2h), 1, "e4m3").T) + f64(b_h2h)
    x = layer_norm_1d(i2h, f64(ln_i2h_w), f64(ln_i2h_b)) + layer_norm_1d(h2h, f64(ln_h2h_w), f64(ln_h2h_b))
    g_i, g_f, g_o, g_c = np.split(x, 4, axis=1)
    in_gate = sigmoid(g_i)
    forget_gate = sigmoid(g_f + FORGET_GATE_BIAS)
    out_gate = sigmoid(g_o)
    in_transform = np.tanh(g_c)
    cx_new = forget_gate * f64(cx) + in_gate * in_transform
    hx_new = out_gate * np.tanh(layer_norm_1d(cx_new, f64(ln_h2o_w), f64(ln_h2o_b)))
    return hx_new, cx_new

@@ -1,0 +1,386 @@
+from contextlib import ExitStack
+
+import concourse.masks as masks
+import concourse.mybir as mybir
+
+F32 = mybir.dt.float32
+BF16 = mybir.dt.bfloat16
+U32 = mybir.dt.uint32
+U8 = mybir.dt.uint8
+FP8X4 = mybir.dt.float8_e4m3fn_x4
+ALU = mybir.AluOpType
+ACT = mybir.ActivationFunctionType
+AX = mybir.AxisListType
+
+P = 128
+B = 512
+K = 1024
+H = 1024
+G4 = 4 * H
+RT = B // P
+CH = 512
+NCH = G4 // CH
+EPS = 1e-5
+
+FLOPS = 2 * 2 * B * K * G4
+
+
+def tile_layernormlstmcell_kernel(
+    tc, inputs, hx, cx, w_i2h, b_i2h, w_h2h, b_h2h,
+    ln_i2h_w, ln_i2h_b, ln_h2h_w, ln_h2h_b, ln_h2o_w, ln_h2o_b, out_0, out_1,
+):
+    nc = tc.nc
+    acts = [inputs, hx]
+    weights = [w_i2h, w_h2h]
+    biases = [b_i2h, b_h2h]
+
+    with ExitStack() as ctx:
+        const = ctx.enter_context(tc.tile_pool(name="const", bufs=1))
+        stage = ctx.enter_context(tc.tile_pool(name="stage", bufs=2))
+        psum = ctx.enter_context(tc.psum_pool(name="psum", bufs=4))
+
+        ident_f = const.tile([P, P], F32, name="ident_f")
+        masks.make_identity(nc, ident_f[:])
+        ident_b = const.tile([P, P], BF16, name="ident_b")
+        masks.make_identity(nc, ident_b[:])
+
+        half = const.tile([P, RT], F32, name="half")
+        nc.vector.memset(half[:], 0.5)
+        negone = const.tile([P, 1], F32, name="negone")
+        nc.vector.memset(negone[:], -1.0)
+
+        acodes = [const.tile([P, 2 * B], U32, name="acodes%d" % m, align_bytes=64) for m in range(2)]
+        ascales = [const.tile([P, 2 * B], U8, name="ascales%d" % m, align_bytes=64) for m in range(2)]
+        va = [const.tile([P, RT, G4], F32, name="va%d" % m) for m in range(2)]
+        w3bc = const.tile([P, H], BF16, name="w3bc")
+        b3bc = const.tile([P, H], BF16, name="b3bc")
+        cx_sb = const.tile([P, RT, H], BF16, name="cx_sb")
+
+        sums = const.tile([P, 2 * RT * NCH], F32, name="sums")
+        sqs = const.tile([P, 2 * RT * NCH], F32, name="sqs")
+        shift = [const.tile([P, RT], F32, name="shift%d" % m) for m in range(2)]
+        rinv = [const.tile([P, RT], F32, name="rinv%d" % m) for m in range(2)]
+        negmean = [const.tile([P, RT], F32, name="negmean%d" % m) for m in range(2)]
+        nbias = [const.tile([P, RT], F32, name="nbias%d" % m) for m in range(2)]
+
+        vcf = const.tile([P, P], F32, name="vcf")
+        lbc = const.tile([P, 32], F32, name="lbc")
+        vr = const.tile([P, P], BF16, name="vr")
+        nc.scalar.dma_start(out=vr[0:32, :], in_=ln_i2h_w.rearrange("o (t j) -> (o t) j", j=P))
+        nc.scalar.dma_start(out=vr[32:64, :], in_=ln_h2h_w.rearrange("o (t j) -> (o t) j", j=P))
+        nc.scalar.dma_start(out=vr[64:96, :], in_=ln_i2h_b.rearrange("o (t j) -> (o t) j", j=P))
+        nc.scalar.dma_start(out=vr[96:128, :], in_=ln_h2h_b.rearrange("o (t j) -> (o t) j", j=P))
+
+        def vecs():
+            vps = psum.tile([P, P], BF16, tag="tp", name="vps")
+            nc.tensor.transpose(vps[:], vr[:], ident_b[:])
+            nc.vector.tensor_copy(out=vcf[:], in_=vps[:])
+            nc.vector.tensor_tensor(out=lbc[:], in0=vcf[:, 64:96], in1=vcf[:, 96:128], op=ALU.add)
+
+        def prep_load(rows, pieces=1):
+            raw = stage.tile([P, 4, K], BF16, tag="raw", bufs=3, name="raw")
+            step = 4 // pieces
+            for t in range(0, 4, step):
+                nc.sync.dma_start(
+                    out=raw[:, t:t + step, :],
+                    in_=rows[t * P:(t + step) * P, :].rearrange("(t p) k -> p t k", p=P),
+                )
+            grouped = stage.tile([P, 2048], F32, tag="grouped", name="grouped", align_bytes=64)
+            return raw, grouped
+
+        def prep_half(loaded, codes, scales, g):
+            raw, grouped = loaded
+            gview = grouped[:].rearrange("p (g j u) -> p g j u", g=2, u=2)
+            for hf in range(2):
+                tp = psum.tile([P, 2, 256], F32, tag="tp", name="tp")
+                for u in range(2):
+                    for tt in range(2):
+                        nc.tensor.transpose(
+                            tp[:, u, tt * P:(tt + 1) * P],
+                            raw[:, 2 * hf + tt, :].bitcast(F32)[:, 256 * g + u:256 * (g + 1):2],
+                            ident_f[:],
+                        )
+                if g == 1 and hf == 1:
+                    nc.vector.tensor_copy(
+                        out=gview[:, g, hf * 256:(hf + 1) * 256, :],
+                        in_=tp[:].rearrange("p u j -> p j u"),
+                    )
+                else:
+                    nc.scalar.copy(
+                        out=gview[:, g, hf * 256:(hf + 1) * 256, :],
+                        in_=tp[:].rearrange("p u j -> p j u"),
+                    )
+            nc.vector.quantize_mx(
+                out=codes[:, g * 512:(g + 1) * 512].bitcast(FP8X4),
+                scales=scales[:, g * 512:(g + 1) * 512],
+                in_=grouped[:, g * 1024:(g + 1) * 1024].bitcast(BF16),
+            )
+
+        def prep(rows, codes, scales, pieces=1):
+            loaded = prep_load(rows, pieces)
+            prep_half(loaded, codes, scales, 0)
+            prep_half(loaded, codes, scales, 1)
+
+        def load_w(idx):
+            m, c = divmod(idx, NCH)
+            wcodes = stage.tile([P, 1024], U32, tag="wcodes", name="wcodes", align_bytes=64)
+            wscales = stage.tile([P, 1024], U8, tag="wscales", name="wscales", align_bytes=64)
+            loaded = prep_load(weights[m][c * CH:(c + 1) * CH, :], pieces=(2 if idx == 0 else 1))
+            bbc = stage.tile([P, CH], BF16, tag="bbc", bufs=3, name="bbc")
+            nc.sync.dma_start(out=bbc[:], in_=biases[m][c * CH:(c + 1) * CH].partition_broadcast(P))
+            return loaded, (wcodes, wscales, bbc)
+
+        def mx_rows(idx, ops, row_tiles):
+            m, c = divmod(idx, NCH)
+            wcodes, wscales, bbc = ops
+            cols = slice(c * CH, (c + 1) * CH)
+            for r in row_tiles:
+                acc = psum.tile([P, CH], F32, tag="acc", name="acc")
+                for g in range(2):
+                    a_cols = slice(g * B + r * P, g * B + (r + 1) * P)
+                    w_cols = slice(g * CH, (g + 1) * CH)
+                    nc.tensor.matmul_mx(
+                        out=acc[:],
+                        lhsT=acodes[m][:, a_cols].bitcast(FP8X4),
+                        lhsT_scale=ascales[m][:, a_cols],
+                        rhs=wcodes[:, w_cols].bitcast(FP8X4),
+                        rhs_scale=wscales[:, w_cols],
+                        start=(g == 0),
+                        stop=(g == 1),
+                    )
+                k = (m * RT + r) * NCH + c
+                nc.vector.scalar_tensor_tensor(
+                    out=va[m][:, r, cols], in0=acc[:], scalar=1.0, in1=bbc[:],
+                    op0=ALU.mult, op1=ALU.add, accum_out=sums[:, k:k + 1],
+                )
+
+        def squares(idx):
+            m, c = divmod(idx, NCH)
+            cols = slice(c * CH, (c + 1) * CH)
+            if c == 0:
+                first = sums[:, m * RT * NCH:(m + 1) * RT * NCH].rearrange("p (r c) -> p r c", c=NCH)[:, :, 0]
+                nc.vector.tensor_scalar(
+                    out=shift[m][:], in0=first, scalar1=-1.0 / CH, scalar2=None, op0=ALU.mult,
+                )
+            for r in range(RT):
+                k = (m * RT + r) * NCH + c
+                junk = stage.tile([P, CH], BF16, tag="junk", name="junk")
+                nc.scalar.activation(
+                    out=junk[:], in_=va[m][:, r, cols], func=ACT.Square,
+                    bias=shift[m][:, r:r + 1], scale=1.0, accum_out=sqs[:, k:k + 1],
+                )
+
+        def small(name):
+            return const.tile([P, RT], F32, name=name)
+
+        stat_std = [small("std_%d" % m) for m in range(2)]
+
+        def stats_a(m):
+            n = float(G4)
+            seg = slice(m * RT * NCH, (m + 1) * RT * NCH)
+            s1 = small("s1_%d" % m)
+            nc.vector.tensor_reduce(out=s1[:], in_=sums[:, seg].rearrange("p (r c) -> p r c", c=NCH), axis=AX.X, op=ALU.add)
+            q1 = small("q1_%d" % m)
+            nc.vector.tensor_reduce(out=q1[:], in_=sqs[:, seg].rearrange("p (r c) -> p r c", c=NCH), axis=AX.X, op=ALU.add)
+            nc.vector.tensor_scalar(out=negmean[m][:], in0=s1[:], scalar1=-1.0 / n, scalar2=None, op0=ALU.mult)
+            d = small("d_%d" % m)
+            nc.vector.tensor_tensor(out=d[:], in0=shift[m][:], in1=negmean[m][:], op=ALU.subtract)
+            d2 = small("d2_%d" % m)
+            nc.vector.scalar_tensor_tensor(out=d2[:], in0=d[:], scalar=n, in1=d[:], op0=ALU.mult, op1=ALU.mult)
+            var = small("var_%d" % m)
+            nc.vector.tensor_tensor(out=var[:], in0=q1[:], in1=d2[:], op=ALU.subtract)
+            nc.vector.tensor_scalar(out=var[:], in0=var[:], scalar1=1.0 / (n - 1.0), scalar2=0.0, op0=ALU.mult, op1=ALU.max)
+            nc.gpsimd.tensor_tensor(out=stat_std[m][:], in0=var[:], in1=half[:], op=ALU.pow)
+
+        def stats_b(m):
+            std = stat_std[m]
+            nc.vector.tensor_scalar(out=std[:], in0=std[:], scalar1=EPS, scalar2=None, op0=ALU.add)
+            nc.vector.reciprocal(out=rinv[m][:], in_=std[:])
+            nc.vector.tensor_tensor(out=nbias[m][:], in0=negmean[m][:], in1=rinv[m][:], op=ALU.mult)
+
+        def norm(m, gate, on_scalar):
+            cols = slice(gate * H, (gate + 1) * H)
+            for r in range(RT):
+                if r in on_scalar:
+                    nc.scalar.activation(
+                        out=va[m][:, r, cols], in_=va[m][:, r, cols], func=ACT.Identity,
+                        scale=rinv[m][:, r:r + 1], bias=nbias[m][:, r:r + 1],
+                    )
+                else:
+                    nc.vector.tensor_scalar(
+                        out=va[m][:, r, cols], in0=va[m][:, r, cols],
+                        scalar1=negmean[m][:, r:r + 1], scalar2=rinv[m][:, r:r + 1],
+                        op0=ALU.add, op1=ALU.mult,
+                    )
+
+        def fa(q):
+            for jt in range(4 * q, 4 * q + 4):
+                cols = slice(jt * P, (jt + 1) * P)
+                pf = psum.tile([P, RT, P], F32, tag="tp", name="pf")
+                for r in range(RT):
+                    nc.tensor.transpose(pf[:, r, :], va[0][:, r, cols], ident_f[:])
+                nc.scalar.activation(
+                    out=va[0][:, :, cols], in_=pf[:], func=ACT.Identity,
+                    scale=vcf[:, jt:jt + 1], bias=lbc[:, jt:jt + 1],
+                )
+
+        def fb(q):
+            for jt in range(4 * q, 4 * q + 4):
+                cols = slice(jt * P, (jt + 1) * P)
+                pf = psum.tile([P, RT, P], F32, tag="tp", name="pf")
+                for r in range(RT):
+                    nc.tensor.transpose(pf[:, r, :], va[1][:, r, cols], ident_f[:])
+                nc.vector.scalar_tensor_tensor(
+                    out=va[0][:, :, cols], in0=pf[:], scalar=vcf[:, 32 + jt:33 + jt], in1=va[0][:, :, cols],
+                    op0=ALU.mult, op1=ALU.add,
+                )
+
+        def bphase(q):
+            gate = q // 2
+            cols = slice(q * CH, (q + 1) * CH)
+            for r in range(RT):
+                pb = psum.tile([P, CH], F32, tag="acc", name="pb")
+                for t in range(4):
+                    jt = 4 * q + t
+                    nc.tensor.transpose(pb[:, t * P:(t + 1) * P], va[0][:, r, jt * P:(jt + 1) * P], ident_f[:])
+                if gate == 1:
+                    nc.scalar.activation(out=va[1][:, r, cols], in_=pb[:], func=ACT.Sigmoid, bias=negone[:, 0:1], scale=1.0)
+                elif gate == 3:
+                    nc.scalar.activation(out=va[1][:, r, cols], in_=pb[:], func=ACT.Tanh)
+                else:
+                    nc.scalar.activation(out=va[1][:, r, cols], in_=pb[:], func=ACT.Sigmoid)
+
+        prep(acts[0], acodes[0], ascales[0], pieces=4)
+        loaded, nxt = load_w(0)
+        prep_half(loaded, nxt[0], nxt[1], 0)
+        prep_half(loaded, nxt[0], nxt[1], 1)
+        for idx in range(2 * NCH):
+            cur = nxt
+            if idx == NCH - 2:
+                prep(acts[1], acodes[1], ascales[1])
+            if idx == NCH + 2:
+                nc.sync.dma_start(out=cx_sb[:], in_=cx.rearrange("(r p) h -> p r h", p=P))
+                nc.sync.dma_start(out=w3bc[:], in_=ln_h2o_w.rearrange("o n -> (o n)").partition_broadcast(P))
+                nc.sync.dma_start(out=b3bc[:], in_=ln_h2o_b.rearrange("o n -> (o n)").partition_broadcast(P))
+            more = idx + 1 < 2 * NCH
+            if more:
+                loaded, nxt = load_w(idx + 1)
+                prep_half(loaded, nxt[0], nxt[1], 0)
+            mx_rows(idx, cur, (0, 1))
+            if more:
+                prep_half(loaded, nxt[0], nxt[1], 1)
+            mx_rows(idx, cur, (2, 3))
+            squares(idx)
+            if idx == NCH:
+                stats_a(0)
+            if idx == NCH + 1:
+                stats_b(0)
+            if idx == 2:
+                vecs()
+            if idx in (NCH + 2, NCH + 4):
+                norm(0, (1, 0)[(idx - NCH - 2) // 2], (3,))
+        fa(2)
+        fa(0)
+        stats_a(1)
+        norm(0, 3, (3,))
+        fa(6)
+        stats_b(1)
+
+        s3 = const.tile([P, RT], F32, name="s3")
+        q3 = const.tile([P, RT], F32, name="q3")
+        negm3 = const.tile([P, RT], F32, name="negm3")
+        r3 = const.tile([P, RT], F32, name="r3")
+
+        def parts(r):
+            return (va[1][:, r, 0:H], va[1][:, r, H:2 * H], va[1][:, r, 2 * H:3 * H], va[1][:, r, 3 * H:4 * H],
+                    va[0][:, r, 0:H], va[0][:, r, H:2 * H], va[0][:, r, 3 * H:4 * H], va[0][:, r, 2 * H:3 * H])
+
+        s3h = const.tile([P, RT, 2], F32, name="s3h")
+
+        def cab(hf):
+            cc = slice(hf * CH, (hf + 1) * CH)
+            for r in range(RT):
+                gi, gf, go, gc, t0, t1, cn, hn = parts(r)
+                nc.vector.tensor_tensor(out=t0[:, cc], in0=gf[:, cc], in1=cx_sb[:, r, cc], op=ALU.mult)
+                nc.vector.tensor_tensor(out=t1[:, cc], in0=gi[:, cc], in1=gc[:, cc], op=ALU.mult)
+                nc.vector.scalar_tensor_tensor(
+                    out=cn[:, cc], in0=t0[:, cc], scalar=1.0, in1=t1[:, cc], op0=ALU.mult, op1=ALU.add,
+                    accum_out=s3h[:, r, hf:hf + 1],
+                )
+
+        def c3(r):
+            gi, gf, go, gc, t0, t1, cn, hn = parts(r)
+            rr = slice(r, r + 1)
+            nc.sync.dma_start(out=out_1[r * P:(r + 1) * P, :], in_=cn)
+            nc.vector.tensor_tensor(out=s3[:, rr], in0=s3h[:, r, 0:1], in1=s3h[:, r, 1:2], op=ALU.add)
+            nc.vector.tensor_scalar(out=negm3[:, rr], in0=s3[:, rr], scalar1=-1.0 / H, scalar2=None, op0=ALU.mult)
+            nc.scalar.activation(out=t0, in_=cn, func=ACT.Square, bias=negm3[:, rr], scale=1.0, accum_out=q3[:, rr])
+            nc.vector.scalar_tensor_tensor(out=t1, in0=cn, scalar=negm3[:, rr], in1=w3bc[:], op0=ALU.add, op1=ALU.mult)
+
+        var3s = [const.tile([P, 1], F32, name="var3_%d" % r) for r in range(RT)]
+        std3s = [const.tile([P, 1], F32, name="std3_%d" % r) for r in range(RT)]
+
+        def fin1a(r):
+            rr = slice(r, r + 1)
+            nc.vector.tensor_scalar(out=var3s[r][:], in0=q3[:, rr], scalar1=1.0 / (H - 1.0), scalar2=None, op0=ALU.mult)
+            nc.gpsimd.tensor_tensor(out=std3s[r][:], in0=var3s[r][:], in1=half[:, 0:1], op=ALU.pow)
+
+        def fin1b(r):
+            gi, gf, go, gc, t0, t1, cn, hn = parts(r)
+            rr = slice(r, r + 1)
+            var3 = var3s[r]
+            std3 = std3s[r]
+            nc.vector.tensor_scalar(out=var3[:], in0=std3[:], scalar1=EPS, scalar2=None, op0=ALU.add)
+            nc.vector.reciprocal(out=r3[:, rr], in_=var3[:])
+            nc.vector.scalar_tensor_tensor(out=t1, in0=t1, scalar=r3[:, rr], in1=b3bc[:], op0=ALU.mult, op1=ALU.add)
+            nc.scalar.activation(out=t1, in_=t1, func=ACT.Tanh)
+
+        def fin2(r):
+            gi, gf, go, gc, t0, t1, cn, hn = parts(r)
+            nc.vector.tensor_tensor(out=hn, in0=go, in1=t1, op=ALU.mult)
+            nc.sync.dma_start(out=out_0[r * P:(r + 1) * P, :], in_=hn)
+
+        norm(1, 1, (2, 3))
+        norm(1, 0, (2, 3))
+        fb(2)
+        norm(1, 3, (2, 3))
+        fb(0)
+        bphase(2)
+        fb(6)
+        bphase(0)
+        norm(0, 2, (3,))
+        fa(3)
+        fb(3)
+        bphase(6)
+        cab(0)
+        fa(1)
+        fb(1)
+        bphase(3)
+        norm(1, 2, (3,))
+        fa(7)
+        fb(7)
+        bphase(1)
+        fa(4)
+        fb(4)
+        bphase(7)
+        cab(1)
+        fa(5)
+        fb(5)
+        c3(0)
+        c3(1)
+        fin1a(0)
+        bphase(4)
+        c3(2)
+        fin1a(1)
+        fin1b(0)
+        c3(3)
+        fin1a(2)
+        fin1b(1)
+        bphase(5)
+        fin2(0)
+        fin1a(3)
+        fin1b(2)
+        fin2(1)
+        fin1b(3)
+        fin2(2)
+        fin2(3)

@@ -88,7 +88,7 @@ def tile_layernormlstmcell_kernel(
             grouped = stage.tile([P, 2048], F32, tag="grouped", name="grouped", align_bytes=64)
             return raw, grouped
 
-        def prep_half(loaded, codes, scales, g):
+        def prep_half(loaded, codes, scales, g, vector_copies=((1, 1),)):
             raw, grouped = loaded
             gview = grouped[:].rearrange("p (g j u) -> p g j u", g=2, u=2)
             for hf in range(2):
@@ -100,7 +100,7 @@ def tile_layernormlstmcell_kernel(
                             raw[:, 2 * hf + tt, :].bitcast(F32)[:, 256 * g + u:256 * (g + 1):2],
                             ident_f[:],
                         )
-                if g == 1 and hf == 1:
+                if (g, hf) in vector_copies:
                     nc.vector.tensor_copy(
                         out=gview[:, g, hf * 256:(hf + 1) * 256, :],
                         in_=tp[:].rearrange("p u j -> p j u"),
@@ -116,8 +116,8 @@ def tile_layernormlstmcell_kernel(
                 in_=grouped[:, g * 1024:(g + 1) * 1024].bitcast(BF16),
             )
 
-        def prep(rows, codes, scales, pieces=1):
-            loaded = prep_load(rows, pieces)
+        def prep(rows, codes, scales):
+            loaded = prep_load(rows)
             prep_half(loaded, codes, scales, 0)
             prep_half(loaded, codes, scales, 1)
 
@@ -198,18 +198,27 @@ def tile_layernormlstmcell_kernel(
             nc.vector.reciprocal(out=rinv[m][:], in_=std[:])
             nc.vector.tensor_tensor(out=nbias[m][:], in0=negmean[m][:], in1=rinv[m][:], op=ALU.mult)
 
-        def norm(m, gate, on_scalar):
-            cols = slice(gate * H, (gate + 1) * H)
+        def norm_gpsimd(m, q):
+            cols = slice(q * CH, (q + 1) * CH)
+            for r in range(RT):
+                nc.gpsimd.tensor_scalar(
+                    out=va[m][:, r, cols], in0=va[m][:, r, cols],
+                    scalar1=negmean[m][:, r:r + 1], scalar2=rinv[m][:, r:r + 1],
+                    op0=ALU.add, op1=ALU.mult,
+                )
+
+        def norm1(q, on_scalar):
+            cols = slice(q * CH, (q + 1) * CH)
             for r in range(RT):
                 if r in on_scalar:
                     nc.scalar.activation(
-                        out=va[m][:, r, cols], in_=va[m][:, r, cols], func=ACT.Identity,
-                        scale=rinv[m][:, r:r + 1], bias=nbias[m][:, r:r + 1],
+                        out=va[1][:, r, cols], in_=va[1][:, r, cols], func=ACT.Identity,
+                        scale=rinv[1][:, r:r + 1], bias=nbias[1][:, r:r + 1],
                     )
                 else:
                     nc.vector.tensor_scalar(
-                        out=va[m][:, r, cols], in0=va[m][:, r, cols],
-                        scalar1=negmean[m][:, r:r + 1], scalar2=rinv[m][:, r:r + 1],
+                        out=va[1][:, r, cols], in0=va[1][:, r, cols],
+                        scalar1=negmean[1][:, r:r + 1], scalar2=rinv[1][:, r:r + 1],
                         op0=ALU.add, op1=ALU.mult,
                     )
 
@@ -250,10 +259,11 @@ def tile_layernormlstmcell_kernel(
                 else:
                     nc.scalar.activation(out=va[1][:, r, cols], in_=pb[:], func=ACT.Sigmoid)
 
-        prep(acts[0], acodes[0], ascales[0], pieces=4)
+        first = prep_load(acts[0], pieces=4)
         loaded, nxt = load_w(0)
-        prep_half(loaded, nxt[0], nxt[1], 0)
-        prep_half(loaded, nxt[0], nxt[1], 1)
+        for part, codes, scales in ((first, acodes[0], ascales[0]), (loaded, nxt[0], nxt[1])):
+            for g in range(2):
+                prep_half(part, codes, scales, g, vector_copies=((0, 1), (1, 1)))
         for idx in range(2 * NCH):
             cur = nxt
             if idx == NCH - 2:
@@ -277,12 +287,12 @@ def tile_layernormlstmcell_kernel(
                 stats_b(0)
             if idx == 2:
                 vecs()
-            if idx in (NCH + 2, NCH + 4):
-                norm(0, (1, 0)[(idx - NCH - 2) // 2], (3,))
+            if idx in (NCH + 2, NCH + 3, NCH + 4, NCH + 5):
+                for q in ((2, 3), (0, 1), (6, 7), (4, 5))[idx - NCH - 2]:
+                    norm_gpsimd(0, q)
         fa(2)
         fa(0)
         stats_a(1)
-        norm(0, 3, (3,))
         fa(6)
         stats_b(1)
 
@@ -340,15 +350,15 @@ def tile_layernormlstmcell_kernel(
             nc.vector.tensor_tensor(out=hn, in0=go, in1=t1, op=ALU.mult)
             nc.sync.dma_start(out=out_0[r * P:(r + 1) * P, :], in_=hn)
 
-        norm(1, 1, (2, 3))
-        norm(1, 0, (2, 3))
+        norm1(2, (3,))
+        for q in (6, 3, 1, 7, 4, 5):
+            norm_gpsimd(1, q)
+        norm1(0, (3,))
         fb(2)
-        norm(1, 3, (2, 3))
         fb(0)
         bphase(2)
         fb(6)
         bphase(0)
-        norm(0, 2, (3,))
         fa(3)
         fb(3)
         bphase(6)
@@ -356,7 +366,6 @@ def tile_layernormlstmcell_kernel(
         fa(1)
         fb(1)
         bphase(3)
-        norm(1, 2, (3,))
         fa(7)
         fb(7)
         bphase(1)

@@ -52,8 +52,6 @@ def tile_layernormlstmcell_kernel(
         acodes = [const.tile([P, 2 * B], U32, name="acodes%d" % m, align_bytes=64) for m in range(2)]
         ascales = [const.tile([P, 2 * B], U8, name="ascales%d" % m, align_bytes=64) for m in range(2)]
         va = [const.tile([P, RT, G4], F32, name="va%d" % m) for m in range(2)]
-        w3bc = const.tile([P, H], BF16, name="w3bc")
-        b3bc = const.tile([P, H], BF16, name="b3bc")
         cx_sb = const.tile([P, RT, H], BF16, name="cx_sb")
 
         sums = const.tile([P, 2 * RT * NCH], F32, name="sums")
@@ -71,10 +69,16 @@ def tile_layernormlstmcell_kernel(
         nc.scalar.dma_start(out=vr[64:96, :], in_=ln_i2h_b.rearrange("o (t j) -> (o t) j", j=P))
         nc.scalar.dma_start(out=vr[96:128, :], in_=ln_h2h_b.rearrange("o (t j) -> (o t) j", j=P))
 
+        vr3 = const.tile([P, P], BF16, name="vr3")
+        nc.vector.memset(vr3[:], 0.0)
+        vcf3 = const.tile([P, 16], F32, name="vcf3")
+
         def vecs():
-            vps = psum.tile([P, P], BF16, tag="tp", name="vps")
-            nc.tensor.transpose(vps[:], vr[:], ident_b[:])
-            nc.vector.tensor_copy(out=vcf[:], in_=vps[:])
+            vps = psum.tile([P, 2, P], BF16, tag="tp", name="vps")
+            nc.tensor.transpose(vps[:, 0, :], vr[:], ident_b[:])
+            nc.tensor.transpose(vps[:, 1, :], vr3[:], ident_b[:])
+            nc.vector.tensor_copy(out=vcf[:], in_=vps[:, 0, :])
+            nc.vector.tensor_copy(out=vcf3[:], in_=vps[:, 1, 0:16])
             nc.vector.tensor_tensor(out=lbc[:], in0=vcf[:, 64:96], in1=vcf[:, 96:128], op=ALU.add)
 
         def prep_load(rows, pieces=1):
@@ -222,21 +226,33 @@ def tile_layernormlstmcell_kernel(
                         op0=ALU.add, op1=ALU.mult,
                     )
 
-        def fa(q):
+        def warm(bank, i):
+            if i % 2 == 0:
+                nc.tensor.matmul(bank, lhsT=ident_b[:], rhs=cx_sb[:, 0, 0:CH], start=True, stop=True)
+
+        def fa(q, on_vector=()):
             for jt in range(4 * q, 4 * q + 4):
                 cols = slice(jt * P, (jt + 1) * P)
                 pf = psum.tile([P, RT, P], F32, tag="tp", name="pf")
+                warm(pf[:].rearrange("p r j -> p (r j)"), jt)
                 for r in range(RT):
                     nc.tensor.transpose(pf[:, r, :], va[0][:, r, cols], ident_f[:])
-                nc.scalar.activation(
-                    out=va[0][:, :, cols], in_=pf[:], func=ACT.Identity,
-                    scale=vcf[:, jt:jt + 1], bias=lbc[:, jt:jt + 1],
-                )
+                if jt % 4 in on_vector:
+                    nc.vector.tensor_scalar(
+                        out=va[0][:, :, cols], in0=pf[:], scalar1=vcf[:, jt:jt + 1], scalar2=lbc[:, jt:jt + 1],
+                        op0=ALU.mult, op1=ALU.add,
+                    )
+                else:
+                    nc.scalar.activation(
+                        out=va[0][:, :, cols], in_=pf[:], func=ACT.Identity,
+                        scale=vcf[:, jt:jt + 1], bias=lbc[:, jt:jt + 1],
+                    )
 
         def fb(q):
             for jt in range(4 * q, 4 * q + 4):
                 cols = slice(jt * P, (jt + 1) * P)
                 pf = psum.tile([P, RT, P], F32, tag="tp", name="pf")
+                warm(pf[:].rearrange("p r j -> p (r j)"), jt)
                 for r in range(RT):
                     nc.tensor.transpose(pf[:, r, :], va[1][:, r, cols], ident_f[:])
                 nc.vector.scalar_tensor_tensor(
@@ -249,6 +265,7 @@ def tile_layernormlstmcell_kernel(
             cols = slice(q * CH, (q + 1) * CH)
             for r in range(RT):
                 pb = psum.tile([P, CH], F32, tag="acc", name="pb")
+                warm(pb[:], r)
                 for t in range(4):
                     jt = 4 * q + t
                     nc.tensor.transpose(pb[:, t * P:(t + 1) * P], va[0][:, r, jt * P:(jt + 1) * P], ident_f[:])
@@ -270,8 +287,6 @@ def tile_layernormlstmcell_kernel(
                 prep(acts[1], acodes[1], ascales[1])
             if idx == NCH + 2:
                 nc.sync.dma_start(out=cx_sb[:], in_=cx.rearrange("(r p) h -> p r h", p=P))
-                nc.sync.dma_start(out=w3bc[:], in_=ln_h2o_w.rearrange("o n -> (o n)").partition_broadcast(P))
-                nc.sync.dma_start(out=b3bc[:], in_=ln_h2o_b.rearrange("o n -> (o n)").partition_broadcast(P))
             more = idx + 1 < 2 * NCH
             if more:
                 loaded, nxt = load_w(idx + 1)
@@ -285,15 +300,19 @@ def tile_layernormlstmcell_kernel(
                 stats_a(0)
             if idx == NCH + 1:
                 stats_b(0)
-            if idx == 2:
+            if idx == 1:
+                nc.sync.dma_start(out=vr3[0:8, :], in_=ln_h2o_w.rearrange("o (t j) -> (o t) j", j=P))
+                nc.sync.dma_start(out=vr3[8:16, :], in_=ln_h2o_b.rearrange("o (t j) -> (o t) j", j=P))
+            if idx == 3:
                 vecs()
             if idx in (NCH + 2, NCH + 3, NCH + 4, NCH + 5):
                 for q in ((2, 3), (0, 1), (6, 7), (4, 5))[idx - NCH - 2]:
                     norm_gpsimd(0, q)
-        fa(2)
-        fa(0)
+        fa(2, on_vector=(1, 3))
+        fa(0, on_vector=(1, 3))
         stats_a(1)
-        fa(6)
+        fa(6, on_vector=(1, 3))
+        fa(3, on_vector=(1, 3))
         stats_b(1)
 
         s3 = const.tile([P, RT], F32, name="s3")
@@ -318,39 +337,57 @@ def tile_layernormlstmcell_kernel(
                     accum_out=s3h[:, r, hf:hf + 1],
                 )
 
-        def c3(r):
-            gi, gf, go, gc, t0, t1, cn, hn = parts(r)
-            rr = slice(r, r + 1)
-            nc.sync.dma_start(out=out_1[r * P:(r + 1) * P, :], in_=cn)
-            nc.vector.tensor_tensor(out=s3[:, rr], in0=s3h[:, r, 0:1], in1=s3h[:, r, 1:2], op=ALU.add)
+        def ln3_sums(h):
+            rr = slice(2 * h, 2 * h + 2)
+            nc.vector.tensor_tensor(out=s3[:, rr], in0=s3h[:, rr, 0], in1=s3h[:, rr, 1], op=ALU.add)
             nc.vector.tensor_scalar(out=negm3[:, rr], in0=s3[:, rr], scalar1=-1.0 / H, scalar2=None, op0=ALU.mult)
-            nc.scalar.activation(out=t0, in_=cn, func=ACT.Square, bias=negm3[:, rr], scale=1.0, accum_out=q3[:, rr])
-            nc.vector.scalar_tensor_tensor(out=t1, in0=cn, scalar=negm3[:, rr], in1=w3bc[:], op0=ALU.add, op1=ALU.mult)
+            for r in (2 * h, 2 * h + 1):
+                gi, gf, go, gc, t0, t1, cn, hn = parts(r)
+                nc.sync.dma_start(out=out_1[r * P:(r + 1) * P, :], in_=cn)
+                junk = stage.tile([P, H], BF16, tag="junk3", name="junk3")
+                nc.scalar.activation(out=junk[:], in_=cn, func=ACT.Square, bias=negm3[:, r:r + 1], scale=1.0, accum_out=q3[:, r:r + 1])
+            nc.vector.tensor_scalar(out=var3[h][:], in0=q3[:, rr], scalar1=1.0 / (H - 1.0), scalar2=None, op0=ALU.mult)
+            nc.gpsimd.tensor_tensor(out=std3[h][:], in0=var3[h][:], in1=half[:, 0:2], op=ALU.pow)
 
-        var3s = [const.tile([P, 1], F32, name="var3_%d" % r) for r in range(RT)]
-        std3s = [const.tile([P, 1], F32, name="std3_%d" % r) for r in range(RT)]
+        var3 = [const.tile([P, 2], F32, name="var3_%d" % h) for h in range(2)]
+        std3 = [const.tile([P, 2], F32, name="std3_%d" % h) for h in range(2)]
 
-        def fin1a(r):
-            rr = slice(r, r + 1)
-            nc.vector.tensor_scalar(out=var3s[r][:], in0=q3[:, rr], scalar1=1.0 / (H - 1.0), scalar2=None, op0=ALU.mult)
-            nc.gpsimd.tensor_tensor(out=std3s[r][:], in0=var3s[r][:], in1=half[:, 0:1], op=ALU.pow)
+        def ln3_norm(h):
+            rr = slice(2 * h, 2 * h + 2)
+            nc.vector.tensor_scalar(out=std3[h][:], in0=std3[h][:], scalar1=EPS, scalar2=None, op0=ALU.add)
+            nc.vector.reciprocal(out=r3[:, rr], in_=std3[h][:])
+            for r in (2 * h, 2 * h + 1):
+                gi, gf, go, gc, t0, t1, cn, hn = parts(r)
+                nc.vector.tensor_scalar(
+                    out=t1, in0=cn, scalar1=negm3[:, r:r + 1], scalar2=r3[:, r:r + 1], op0=ALU.add, op1=ALU.mult,
+                )
 
-        def fin1b(r):
-            gi, gf, go, gc, t0, t1, cn, hn = parts(r)
-            rr = slice(r, r + 1)
-            var3 = var3s[r]
-            std3 = std3s[r]
-            nc.vector.tensor_scalar(out=var3[:], in0=std3[:], scalar1=EPS, scalar2=None, op0=ALU.add)
-            nc.vector.reciprocal(out=r3[:, rr], in_=var3[:])
-            nc.vector.scalar_tensor_tensor(out=t1, in0=t1, scalar=r3[:, rr], in1=b3bc[:], op0=ALU.mult, op1=ALU.add)
-            nc.scalar.activation(out=t1, in_=t1, func=ACT.Tanh)
+        def ln3_tanh(h):
+            for t in range(0, H // P, 2):
+                pf = psum.tile([P, 2, 2, P], F32, tag="tp", name="pf")
+                for i in range(2):
+                    for k in range(2):
+                        nc.tensor.transpose(
+                            pf[:, i, k, :], va[0][:, 2 * h + k, H + (t + i) * P:H + (t + i + 1) * P], ident_f[:],
+                        )
+                for i in range(2):
+                    nc.scalar.activation(
+                        out=va[0][:, 2 * h:2 * h + 2, (t + i) * P:(t + i + 1) * P], in_=pf[:, i, :, :], func=ACT.Tanh,
+                        scale=vcf3[:, t + i:t + i + 1], bias=vcf3[:, 8 + t + i:9 + t + i],
+                    )
 
-        def fin2(r):
-            gi, gf, go, gc, t0, t1, cn, hn = parts(r)
-            nc.vector.tensor_tensor(out=hn, in0=go, in1=t1, op=ALU.mult)
-            nc.sync.dma_start(out=out_0[r * P:(r + 1) * P, :], in_=hn)
+        def fin(h):
+            for r in (2 * h, 2 * h + 1):
+                gi, gf, go, gc, t0, t1, cn, hn = parts(r)
+                for c in range(2):
+                    cc = slice(c * CH, (c + 1) * CH)
+                    pb = psum.tile([P, CH], F32, tag="acc", name="pb")
+                    for t in range(4):
+                        nc.tensor.transpose(pb[:, t * P:(t + 1) * P], t0[:, c * CH + t * P:c * CH + (t + 1) * P], ident_f[:])
+                    nc.vector.tensor_tensor(out=hn[:, cc], in0=go[:, cc], in1=pb[:], op=ALU.mult)
+                nc.sync.dma_start(out=out_0[r * P:(r + 1) * P, :], in_=hn)
 
-        norm1(2, (3,))
+        norm1(2, ())
         for q in (6, 3, 1, 7, 4, 5):
             norm_gpsimd(1, q)
         norm1(0, (3,))
@@ -359,7 +396,6 @@ def tile_layernormlstmcell_kernel(
         bphase(2)
         fb(6)
         bphase(0)
-        fa(3)
         fb(3)
         bphase(6)
         cab(0)
@@ -375,21 +411,13 @@ def tile_layernormlstmcell_kernel(
         cab(1)
         fa(5)
         fb(5)
-        c3(0)
-        c3(1)
-        fin1a(0)
+        ln3_sums(0)
         bphase(4)
-        c3(2)
-        fin1a(1)
-        fin1b(0)
-        c3(3)
-        fin1a(2)
-        fin1b(1)
+        ln3_sums(1)
+        ln3_norm(0)
+        ln3_tanh(0)
         bphase(5)
-        fin2(0)
-        fin1a(3)
-        fin1b(2)
-        fin2(1)
-        fin1b(3)
-        fin2(2)
-        fin2(3)
+        ln3_norm(1)
+        ln3_tanh(1)
+        fin(0)
+        fin(1)

@@ -202,39 +202,30 @@ def tile_layernormlstmcell_kernel(
             nc.vector.reciprocal(out=rinv[m][:], in_=std[:])
             nc.vector.tensor_tensor(out=nbias[m][:], in0=negmean[m][:], in1=rinv[m][:], op=ALU.mult)
 
-        def norm_gpsimd(m, q):
-            cols = slice(q * CH, (q + 1) * CH)
-            for r in range(RT):
-                nc.gpsimd.tensor_scalar(
-                    out=va[m][:, r, cols], in0=va[m][:, r, cols],
-                    scalar1=negmean[m][:, r:r + 1], scalar2=rinv[m][:, r:r + 1],
-                    op0=ALU.add, op1=ALU.mult,
-                )
-
-        def norm1(q, on_scalar):
-            cols = slice(q * CH, (q + 1) * CH)
+        def norm(m, q, width, on_scalar):
+            cols = slice(q * CH, q * CH + width)
             for r in range(RT):
                 if r in on_scalar:
                     nc.scalar.activation(
-                        out=va[1][:, r, cols], in_=va[1][:, r, cols], func=ACT.Identity,
-                        scale=rinv[1][:, r:r + 1], bias=nbias[1][:, r:r + 1],
+                        out=va[m][:, r, cols], in_=va[m][:, r, cols], func=ACT.Identity,
+                        scale=rinv[m][:, r:r + 1], bias=nbias[m][:, r:r + 1],
                     )
                 else:
                     nc.vector.tensor_scalar(
-                        out=va[1][:, r, cols], in0=va[1][:, r, cols],
-                        scalar1=negmean[1][:, r:r + 1], scalar2=rinv[1][:, r:r + 1],
+                        out=va[m][:, r, cols], in0=va[m][:, r, cols],
+                        scalar1=negmean[m][:, r:r + 1], scalar2=rinv[m][:, r:r + 1],
                         op0=ALU.add, op1=ALU.mult,
                     )
 
         def warm(bank, i):
-            if i % 2 == 0:
+            if i == 0:
                 nc.tensor.matmul(bank, lhsT=ident_b[:], rhs=cx_sb[:, 0, 0:CH], start=True, stop=True)
 
         def fa(q, on_vector=()):
             for jt in range(4 * q, 4 * q + 4):
                 cols = slice(jt * P, (jt + 1) * P)
                 pf = psum.tile([P, RT, P], F32, tag="tp", name="pf")
-                warm(pf[:].rearrange("p r j -> p (r j)"), jt)
+                warm(pf[:].rearrange("p r j -> p (r j)"), jt % 2)
                 for r in range(RT):
                     nc.tensor.transpose(pf[:, r, :], va[0][:, r, cols], ident_f[:])
                 if jt % 4 in on_vector:
@@ -252,7 +243,7 @@ def tile_layernormlstmcell_kernel(
             for jt in range(4 * q, 4 * q + 4):
                 cols = slice(jt * P, (jt + 1) * P)
                 pf = psum.tile([P, RT, P], F32, tag="tp", name="pf")
-                warm(pf[:].rearrange("p r j -> p (r j)"), jt)
+                warm(pf[:].rearrange("p r j -> p (r j)"), jt % 2)
                 for r in range(RT):
                     nc.tensor.transpose(pf[:, r, :], va[1][:, r, cols], ident_f[:])
                 nc.vector.scalar_tensor_tensor(
@@ -305,12 +296,12 @@ def tile_layernormlstmcell_kernel(
                 nc.sync.dma_start(out=vr3[8:16, :], in_=ln_h2o_b.rearrange("o (t j) -> (o t) j", j=P))
             if idx == 3:
                 vecs()
-            if idx in (NCH + 2, NCH + 3, NCH + 4, NCH + 5):
-                for q in ((2, 3), (0, 1), (6, 7), (4, 5))[idx - NCH - 2]:
-                    norm_gpsimd(0, q)
+            if idx in (NCH + 2, NCH + 4):
+                norm(0, (2, 0)[(idx - NCH - 2) // 2], H, (3,))
         fa(2, on_vector=(1, 3))
         fa(0, on_vector=(1, 3))
         stats_a(1)
+        norm(0, 6, H, (3,))
         fa(6, on_vector=(1, 3))
         fa(3, on_vector=(1, 3))
         stats_b(1)
@@ -365,6 +356,7 @@ def tile_layernormlstmcell_kernel(
         def ln3_tanh(h):
             for t in range(0, H // P, 2):
                 pf = psum.tile([P, 2, 2, P], F32, tag="tp", name="pf")
+                warm(pf[:].rearrange("p i k j -> p (i k j)"), t % 4)
                 for i in range(2):
                     for k in range(2):
                         nc.tensor.transpose(
@@ -382,29 +374,33 @@ def tile_layernormlstmcell_kernel(
                 for c in range(2):
                     cc = slice(c * CH, (c + 1) * CH)
                     pb = psum.tile([P, CH], F32, tag="acc", name="pb")
+                    warm(pb[:], c)
                     for t in range(4):
                         nc.tensor.transpose(pb[:, t * P:(t + 1) * P], t0[:, c * CH + t * P:c * CH + (t + 1) * P], ident_f[:])
                     nc.vector.tensor_tensor(out=hn[:, cc], in0=go[:, cc], in1=pb[:], op=ALU.mult)
                 nc.sync.dma_start(out=out_0[r * P:(r + 1) * P, :], in_=hn)
 
-        norm1(2, ())
-        for q in (6, 3, 1, 7, 4, 5):
-            norm_gpsimd(1, q)
-        norm1(0, (3,))
+        norm(1, 2, CH, ())
+        norm(1, 0, CH, (3,))
         fb(2)
+        norm(1, 6, H, (3,))
         fb(0)
         bphase(2)
         fb(6)
         bphase(0)
+        norm(1, 3, CH, (3,))
         fb(3)
         bphase(6)
         cab(0)
+        norm(1, 1, CH, (3,))
         fa(1)
         fb(1)
         bphase(3)
         fa(7)
         fb(7)
         bphase(1)
+        norm(0, 4, H, (3,))
+        norm(1, 4, H, (3,))
         fa(4)
         fb(4)
         bphase(7)

@@ -184,13 +184,13 @@ def tile_layernormlstmcell_kernel(
             seg = slice(m * RT * NCH, (m + 1) * RT * NCH)
             s1 = small("s1_%d" % m)
             nc.vector.tensor_reduce(out=s1[:], in_=sums[:, seg].rearrange("p (r c) -> p r c", c=NCH), axis=AX.X, op=ALU.add)
-            q1 = small("q1_%d" % m)
-            nc.vector.tensor_reduce(out=q1[:], in_=sqs[:, seg].rearrange("p (r c) -> p r c", c=NCH), axis=AX.X, op=ALU.add)
             nc.vector.tensor_scalar(out=negmean[m][:], in0=s1[:], scalar1=-1.0 / n, scalar2=None, op0=ALU.mult)
             d = small("d_%d" % m)
             nc.vector.tensor_tensor(out=d[:], in0=shift[m][:], in1=negmean[m][:], op=ALU.subtract)
             d2 = small("d2_%d" % m)
             nc.vector.scalar_tensor_tensor(out=d2[:], in0=d[:], scalar=n, in1=d[:], op0=ALU.mult, op1=ALU.mult)
+            q1 = small("q1_%d" % m)
+            nc.vector.tensor_reduce(out=q1[:], in_=sqs[:, seg].rearrange("p (r c) -> p r c", c=NCH), axis=AX.X, op=ALU.add)
             var = small("var_%d" % m)
             nc.vector.tensor_tensor(out=var[:], in0=q1[:], in1=d2[:], op=ALU.subtract)
             nc.vector.tensor_scalar(out=var[:], in0=var[:], scalar1=1.0 / (n - 1.0), scalar2=0.0, op0=ALU.mult, op1=ALU.max)
@@ -217,15 +217,10 @@ def tile_layernormlstmcell_kernel(
                         op0=ALU.add, op1=ALU.mult,
                     )
 
-        def warm(bank, i):
-            if i == 0:
-                nc.tensor.matmul(bank, lhsT=ident_b[:], rhs=cx_sb[:, 0, 0:CH], start=True, stop=True)
-
         def fa(q, on_vector=()):
             for jt in range(4 * q, 4 * q + 4):
                 cols = slice(jt * P, (jt + 1) * P)
                 pf = psum.tile([P, RT, P], F32, tag="tp", name="pf")
-                warm(pf[:].rearrange("p r j -> p (r j)"), jt % 2)
                 for r in range(RT):
                     nc.tensor.transpose(pf[:, r, :], va[0][:, r, cols], ident_f[:])
                 if jt % 4 in on_vector:
@@ -243,7 +238,6 @@ def tile_layernormlstmcell_kernel(
             for jt in range(4 * q, 4 * q + 4):
                 cols = slice(jt * P, (jt + 1) * P)
                 pf = psum.tile([P, RT, P], F32, tag="tp", name="pf")
-                warm(pf[:].rearrange("p r j -> p (r j)"), jt % 2)
                 for r in range(RT):
                     nc.tensor.transpose(pf[:, r, :], va[1][:, r, cols], ident_f[:])
                 nc.vector.scalar_tensor_tensor(
@@ -256,7 +250,6 @@ def tile_layernormlstmcell_kernel(
             cols = slice(q * CH, (q + 1) * CH)
             for r in range(RT):
                 pb = psum.tile([P, CH], F32, tag="acc", name="pb")
-                warm(pb[:], r)
                 for t in range(4):
                     jt = 4 * q + t
                     nc.tensor.transpose(pb[:, t * P:(t + 1) * P], va[0][:, r, jt * P:(jt + 1) * P], ident_f[:])
@@ -302,12 +295,11 @@ def tile_layernormlstmcell_kernel(
         fa(0, on_vector=(1, 3))
         stats_a(1)
         norm(0, 6, H, (3,))
-        fa(6, on_vector=(1, 3))
-        fa(3, on_vector=(1, 3))
+        fa(6)
+        fa(3)
         stats_b(1)
 
         s3 = const.tile([P, RT], F32, name="s3")
-        q3 = const.tile([P, RT], F32, name="q3")
         negm3 = const.tile([P, RT], F32, name="negm3")
         r3 = const.tile([P, RT], F32, name="r3")
 
@@ -317,29 +309,48 @@ def tile_layernormlstmcell_kernel(
 
         s3h = const.tile([P, RT, 2], F32, name="s3h")
 
-        def cab(hf):
+        def cab(hf, rows):
             cc = slice(hf * CH, (hf + 1) * CH)
-            for r in range(RT):
+            for r in rows:
                 gi, gf, go, gc, t0, t1, cn, hn = parts(r)
                 nc.vector.tensor_tensor(out=t0[:, cc], in0=gf[:, cc], in1=cx_sb[:, r, cc], op=ALU.mult)
                 nc.vector.tensor_tensor(out=t1[:, cc], in0=gi[:, cc], in1=gc[:, cc], op=ALU.mult)
+            for r in rows:
+                gi, gf, go, gc, t0, t1, cn, hn = parts(r)
                 nc.vector.scalar_tensor_tensor(
                     out=cn[:, cc], in0=t0[:, cc], scalar=1.0, in1=t1[:, cc], op0=ALU.mult, op1=ALU.add,
                     accum_out=s3h[:, r, hf:hf + 1],
                 )
 
-        def ln3_sums(h):
+        sh3 = const.tile([P, RT], F32, name="sh3")
+        q3h = const.tile([P, RT, 2], F32, name="q3h")
+
+        def squares3(hf, rows):
+            for r in rows:
+                gi, gf, go, gc, t0, t1, cn, hn = parts(r)
+                junk = stage.tile([P, CH], BF16, tag="junk", name="junk")
+                nc.scalar.activation(
+                    out=junk[:], in_=cn[:, hf * CH:(hf + 1) * CH], func=ACT.Square,
+                    bias=sh3[:, r:r + 1], scale=1.0, accum_out=q3h[:, r, hf:hf + 1],
+                )
+
+        def ln3_stats(h):
             rr = slice(2 * h, 2 * h + 2)
+            for r in (2 * h, 2 * h + 1):
+                nc.sync.dma_start(out=out_1[r * P:(r + 1) * P, :], in_=parts(r)[6])
             nc.vector.tensor_tensor(out=s3[:, rr], in0=s3h[:, rr, 0], in1=s3h[:, rr, 1], op=ALU.add)
             nc.vector.tensor_scalar(out=negm3[:, rr], in0=s3[:, rr], scalar1=-1.0 / H, scalar2=None, op0=ALU.mult)
-            for r in (2 * h, 2 * h + 1):
-                gi, gf, go, gc, t0, t1, cn, hn = parts(r)
-                nc.sync.dma_start(out=out_1[r * P:(r + 1) * P, :], in_=cn)
-                junk = stage.tile([P, H], BF16, tag="junk3", name="junk3")
-                nc.scalar.activation(out=junk[:], in_=cn, func=ACT.Square, bias=negm3[:, r:r + 1], scale=1.0, accum_out=q3[:, r:r + 1])
-            nc.vector.tensor_scalar(out=var3[h][:], in0=q3[:, rr], scalar1=1.0 / (H - 1.0), scalar2=None, op0=ALU.mult)
+            nc.vector.tensor_tensor(out=d3[h][:], in0=sh3[:, rr], in1=negm3[:, rr], op=ALU.subtract)
+            nc.vector.scalar_tensor_tensor(out=d3[h][:], in0=d3[h][:], scalar=float(H), in1=d3[h][:], op0=ALU.mult, op1=ALU.mult)
+            nc.vector.tensor_tensor(out=d3[h][:], in0=q3h[:, rr, 0], in1=d3[h][:], op=ALU.subtract)
+            squares3(1, (2 * h, 2 * h + 1))
+            nc.vector.tensor_tensor(out=var3[h][:], in0=q3h[:, rr, 1], in1=d3[h][:], op=ALU.add)
+            nc.vector.tensor_scalar(
+                out=var3[h][:], in0=var3[h][:], scalar1=1.0 / (H - 1.0), scalar2=0.0, op0=ALU.mult, op1=ALU.max,
+            )
             nc.gpsimd.tensor_tensor(out=std3[h][:], in0=var3[h][:], in1=half[:, 0:2], op=ALU.pow)
 
+        d3 = [const.tile([P, 2], F32, name="d3_%d" % h) for h in range(2)]
         var3 = [const.tile([P, 2], F32, name="var3_%d" % h) for h in range(2)]
         std3 = [const.tile([P, 2], F32, name="std3_%d" % h) for h in range(2)]
 
@@ -356,7 +367,6 @@ def tile_layernormlstmcell_kernel(
         def ln3_tanh(h):
             for t in range(0, H // P, 2):
                 pf = psum.tile([P, 2, 2, P], F32, tag="tp", name="pf")
-                warm(pf[:].rearrange("p i k j -> p (i k j)"), t % 4)
                 for i in range(2):
                     for k in range(2):
                         nc.tensor.transpose(
@@ -374,7 +384,6 @@ def tile_layernormlstmcell_kernel(
                 for c in range(2):
                     cc = slice(c * CH, (c + 1) * CH)
                     pb = psum.tile([P, CH], F32, tag="acc", name="pb")
-                    warm(pb[:], c)
                     for t in range(4):
                         nc.tensor.transpose(pb[:, t * P:(t + 1) * P], t0[:, c * CH + t * P:c * CH + (t + 1) * P], ident_f[:])
                     nc.vector.tensor_tensor(out=hn[:, cc], in0=go[:, cc], in1=pb[:], op=ALU.mult)
@@ -386,34 +395,38 @@ def tile_layernormlstmcell_kernel(
         norm(1, 6, H, (3,))
         fb(0)
         bphase(2)
+        norm(1, 3, CH, (3,))
         fb(6)
         bphase(0)
-        norm(1, 3, CH, (3,))
+        fa(1)
         fb(3)
         bphase(6)
-        cab(0)
         norm(1, 1, CH, (3,))
-        fa(1)
+        cab(0, (0, 1))
         fb(1)
         bphase(3)
         fa(7)
+        cab(0, (2, 3))
         fb(7)
         bphase(1)
+        nc.vector.tensor_scalar(out=sh3[:], in0=s3h[:, :, 0], scalar1=-1.0 / CH, scalar2=None, op0=ALU.mult)
         norm(0, 4, H, (3,))
         norm(1, 4, H, (3,))
         fa(4)
-        fb(4)
         bphase(7)
-        cab(1)
+        squares3(0, range(RT))
+        cab(1, (0, 1))
+        ln3_stats(0)
+        fb(4)
         fa(5)
-        fb(5)
-        ln3_sums(0)
+        cab(1, (2, 3))
+        ln3_stats(1)
         bphase(4)
-        ln3_sums(1)
+        fb(5)
         ln3_norm(0)
         ln3_tanh(0)
         bphase(5)
         ln3_norm(1)
         ln3_tanh(1)
-        fin(0)
-        fin(1)
+        for h in range(2):
+            fin(h)

@@ -53,6 +53,8 @@ def tile_layernormlstmcell_kernel(
         ascales = [const.tile([P, 2 * B], U8, name="ascales%d" % m, align_bytes=64) for m in range(2)]
         va = [const.tile([P, RT, G4], F32, name="va%d" % m) for m in range(2)]
         cx_sb = const.tile([P, RT, H], BF16, name="cx_sb")
+        bbc = const.tile([P, 2, G4], BF16, name="bbc")
+        bias_loads = {0: ((0, 0, 1),), 1: ((0, 1, NCH),), 4: ((1, 0, NCH),)}
 
         sums = const.tile([P, 2 * RT * NCH], F32, name="sums")
         sqs = const.tile([P, 2 * RT * NCH], F32, name="sqs")
@@ -130,13 +132,15 @@ def tile_layernormlstmcell_kernel(
             wcodes = stage.tile([P, 1024], U32, tag="wcodes", name="wcodes", align_bytes=64)
             wscales = stage.tile([P, 1024], U8, tag="wscales", name="wscales", align_bytes=64)
             loaded = prep_load(weights[m][c * CH:(c + 1) * CH, :], pieces=(2 if idx == 0 else 1))
-            bbc = stage.tile([P, CH], BF16, tag="bbc", bufs=3, name="bbc")
-            nc.sync.dma_start(out=bbc[:], in_=biases[m][c * CH:(c + 1) * CH].partition_broadcast(P))
-            return loaded, (wcodes, wscales, bbc)
+            for bm, lo, hi in bias_loads.get(idx, ()):
+                nc.sync.dma_start(
+                    out=bbc[:, bm, lo * CH:hi * CH], in_=biases[bm][lo * CH:hi * CH].partition_broadcast(P),
+                )
+            return loaded, (wcodes, wscales)
 
         def mx_rows(idx, ops, row_tiles):
             m, c = divmod(idx, NCH)
-            wcodes, wscales, bbc = ops
+            wcodes, wscales = ops
             cols = slice(c * CH, (c + 1) * CH)
             for r in row_tiles:
                 acc = psum.tile([P, CH], F32, tag="acc", name="acc")
@@ -154,7 +158,7 @@ def tile_layernormlstmcell_kernel(
                     )
                 k = (m * RT + r) * NCH + c
                 nc.vector.scalar_tensor_tensor(
-                    out=va[m][:, r, cols], in0=acc[:], scalar=1.0, in1=bbc[:],
+                    out=va[m][:, r, cols], in0=acc[:], scalar=1.0, in1=bbc[:, m, cols],
                     op0=ALU.mult, op1=ALU.add, accum_out=sums[:, k:k + 1],
                 )
 

from contextlib import ExitStack

import concourse.masks as masks
import concourse.mybir as mybir

F32 = mybir.dt.float32
BF16 = mybir.dt.bfloat16
U32 = mybir.dt.uint32
U8 = mybir.dt.uint8
FP8X4 = mybir.dt.float8_e4m3fn_x4
ALU = mybir.AluOpType
ACT = mybir.ActivationFunctionType
AX = mybir.AxisListType

P = 128
B = 512
K = 1024
H = 1024
G4 = 4 * H
RT = B // P
CH = 512
NCH = G4 // CH
EPS = 1e-5

FLOPS = 2 * 2 * B * K * G4


def tile_layernormlstmcell_kernel(
    tc, inputs, hx, cx, w_i2h, b_i2h, w_h2h, b_h2h,
    ln_i2h_w, ln_i2h_b, ln_h2h_w, ln_h2h_b, ln_h2o_w, ln_h2o_b, out_0, out_1,
):
    nc = tc.nc
    acts = [inputs, hx]
    weights = [w_i2h, w_h2h]
    biases = [b_i2h, b_h2h]

    with ExitStack() as ctx:
        const = ctx.enter_context(tc.tile_pool(name="const", bufs=1))
        stage = ctx.enter_context(tc.tile_pool(name="stage", bufs=2))
        psum = ctx.enter_context(tc.psum_pool(name="psum", bufs=4))

        ident_f = const.tile([P, P], F32, name="ident_f")
        masks.make_identity(nc, ident_f[:])
        ident_b = const.tile([P, P], BF16, name="ident_b")
        masks.make_identity(nc, ident_b[:])

        half = const.tile([P, RT], F32, name="half")
        nc.vector.memset(half[:], 0.5)
        negone = const.tile([P, 1], F32, name="negone")
        nc.vector.memset(negone[:], -1.0)

        acodes = [const.tile([P, 2 * B], U32, name="acodes%d" % m, align_bytes=64) for m in range(2)]
        ascales = [const.tile([P, 2 * B], U8, name="ascales%d" % m, align_bytes=64) for m in range(2)]
        va = [const.tile([P, RT, G4], F32, name="va%d" % m) for m in range(2)]
        cx_sb = const.tile([P, RT, H], BF16, name="cx_sb")
        bbc = const.tile([P, 2, G4], BF16, name="bbc")
        bias_loads = {0: ((0, 0, 1),), 1: ((0, 1, NCH),), 4: ((1, 0, NCH),)}

        sums = const.tile([P, 2 * RT * NCH], F32, name="sums")
        sqs = const.tile([P, 2 * RT * NCH], F32, name="sqs")
        shift = [const.tile([P, RT], F32, name="shift%d" % m) for m in range(2)]
        rinv = [const.tile([P, RT], F32, name="rinv%d" % m) for m in range(2)]
        negmean = [const.tile([P, RT], F32, name="negmean%d" % m) for m in range(2)]
        nbias = [const.tile([P, RT], F32, name="nbias%d" % m) for m in range(2)]

        vcf = const.tile([P, P], F32, name="vcf")
        lbc = const.tile([P, 32], F32, name="lbc")
        vr = const.tile([P, P], BF16, name="vr")
        nc.scalar.dma_start(out=vr[0:32, :], in_=ln_i2h_w.rearrange("o (t j) -> (o t) j", j=P))
        nc.scalar.dma_start(out=vr[32:64, :], in_=ln_h2h_w.rearrange("o (t j) -> (o t) j", j=P))
        nc.scalar.dma_start(out=vr[64:96, :], in_=ln_i2h_b.rearrange("o (t j) -> (o t) j", j=P))
        nc.scalar.dma_start(out=vr[96:128, :], in_=ln_h2h_b.rearrange("o (t j) -> (o t) j", j=P))

        vr3 = const.tile([P, P], BF16, name="vr3")
        nc.vector.memset(vr3[:], 0.0)
        vcf3 = const.tile([P, 16], F32, name="vcf3")

        def vecs():
            vps = psum.tile([P, 2, P], BF16, tag="tp", name="vps")
            nc.tensor.transpose(vps[:, 0, :], vr[:], ident_b[:])
            nc.tensor.transpose(vps[:, 1, :], vr3[:], ident_b[:])
            nc.vector.tensor_copy(out=vcf[:], in_=vps[:, 0, :])
            nc.vector.tensor_copy(out=vcf3[:], in_=vps[:, 1, 0:16])
            nc.vector.tensor_tensor(out=lbc[:], in0=vcf[:, 64:96], in1=vcf[:, 96:128], op=ALU.add)

        def prep_load(rows, pieces=1):
            raw = stage.tile([P, 4, K], BF16, tag="raw", bufs=3, name="raw")
            step = 4 // pieces
            for t in range(0, 4, step):
                nc.sync.dma_start(
                    out=raw[:, t:t + step, :],
                    in_=rows[t * P:(t + step) * P, :].rearrange("(t p) k -> p t k", p=P),
                )
            grouped = stage.tile([P, 2048], F32, tag="grouped", name="grouped", align_bytes=64)
            return raw, grouped

        def prep_half(loaded, codes, scales, g, vector_copies=((1, 1),)):
            raw, grouped = loaded
            gview = grouped[:].rearrange("p (g j u) -> p g j u", g=2, u=2)
            for hf in range(2):
                tp = psum.tile([P, 2, 256], F32, tag="tp", name="tp")
                for u in range(2):
                    for tt in range(2):
                        nc.tensor.transpose(
                            tp[:, u, tt * P:(tt + 1) * P],
                            raw[:, 2 * hf + tt, :].bitcast(F32)[:, 256 * g + u:256 * (g + 1):2],
                            ident_f[:],
                        )
                if (g, hf) in vector_copies:
                    nc.vector.tensor_copy(
                        out=gview[:, g, hf * 256:(hf + 1) * 256, :],
                        in_=tp[:].rearrange("p u j -> p j u"),
                    )
                else:
                    nc.scalar.copy(
                        out=gview[:, g, hf * 256:(hf + 1) * 256, :],
                        in_=tp[:].rearrange("p u j -> p j u"),
                    )
            nc.vector.quantize_mx(
                out=codes[:, g * 512:(g + 1) * 512].bitcast(FP8X4),
                scales=scales[:, g * 512:(g + 1) * 512],
                in_=grouped[:, g * 1024:(g + 1) * 1024].bitcast(BF16),
            )

        def prep(rows, codes, scales):
            loaded = prep_load(rows)
            prep_half(loaded, codes, scales, 0)
            prep_half(loaded, codes, scales, 1)

        def load_w(idx):
            m, c = divmod(idx, NCH)
            wcodes = stage.tile([P, 1024], U32, tag="wcodes", name="wcodes", align_bytes=64)
            wscales = stage.tile([P, 1024], U8, tag="wscales", name="wscales", align_bytes=64)
            loaded = prep_load(weights[m][c * CH:(c + 1) * CH, :], pieces=(2 if idx == 0 else 1))
            for bm, lo, hi in bias_loads.get(idx, ()):
                nc.sync.dma_start(
                    out=bbc[:, bm, lo * CH:hi * CH], in_=biases[bm][lo * CH:hi * CH].partition_broadcast(P),
                )
            return loaded, (wcodes, wscales)

        def mx_rows(idx, ops, row_tiles):
            m, c = divmod(idx, NCH)
            wcodes, wscales = ops
            cols = slice(c * CH, (c + 1) * CH)
            for r in row_tiles:
                acc = psum.tile([P, CH], F32, tag="acc", name="acc")
                for g in range(2):
                    a_cols = slice(g * B + r * P, g * B + (r + 1) * P)
                    w_cols = slice(g * CH, (g + 1) * CH)
                    nc.tensor.matmul_mx(
                        out=acc[:],
                        lhsT=acodes[m][:, a_cols].bitcast(FP8X4),
                        lhsT_scale=ascales[m][:, a_cols],
                        rhs=wcodes[:, w_cols].bitcast(FP8X4),
                        rhs_scale=wscales[:, w_cols],
                        start=(g == 0),
                        stop=(g == 1),
                    )
                k = (m * RT + r) * NCH + c
                nc.vector.scalar_tensor_tensor(
                    out=va[m][:, r, cols], in0=acc[:], scalar=1.0, in1=bbc[:, m, cols],
                    op0=ALU.mult, op1=ALU.add, accum_out=sums[:, k:k + 1],
                )

        def squares(idx):
            m, c = divmod(idx, NCH)
            cols = slice(c * CH, (c + 1) * CH)
            if c == 0:
                first = sums[:, m * RT * NCH:(m + 1) * RT * NCH].rearrange("p (r c) -> p r c", c=NCH)[:, :, 0]
                nc.vector.tensor_scalar(
                    out=shift[m][:], in0=first, scalar1=-1.0 / CH, scalar2=None, op0=ALU.mult,
                )
            for r in range(RT):
                k = (m * RT + r) * NCH + c
                junk = stage.tile([P, CH], BF16, tag="junk", name="junk")
                nc.scalar.activation(
                    out=junk[:], in_=va[m][:, r, cols], func=ACT.Square,
                    bias=shift[m][:, r:r + 1], scale=1.0, accum_out=sqs[:, k:k + 1],
                )

        def small(name):
            return const.tile([P, RT], F32, name=name)

        stat_std = [small("std_%d" % m) for m in range(2)]

        def stats_a(m):
            n = float(G4)
            seg = slice(m * RT * NCH, (m + 1) * RT * NCH)
            s1 = small("s1_%d" % m)
            nc.vector.tensor_reduce(out=s1[:], in_=sums[:, seg].rearrange("p (r c) -> p r c", c=NCH), axis=AX.X, op=ALU.add)
            nc.vector.tensor_scalar(out=negmean[m][:], in0=s1[:], scalar1=-1.0 / n, scalar2=None, op0=ALU.mult)
            d = small("d_%d" % m)
            nc.vector.tensor_tensor(out=d[:], in0=shift[m][:], in1=negmean[m][:], op=ALU.subtract)
            d2 = small("d2_%d" % m)
            nc.vector.scalar_tensor_tensor(out=d2[:], in0=d[:], scalar=n, in1=d[:], op0=ALU.mult, op1=ALU.mult)
            q1 = small("q1_%d" % m)
            nc.vector.tensor_reduce(out=q1[:], in_=sqs[:, seg].rearrange("p (r c) -> p r c", c=NCH), axis=AX.X, op=ALU.add)
            var = small("var_%d" % m)
            nc.vector.tensor_tensor(out=var[:], in0=q1[:], in1=d2[:], op=ALU.subtract)
            nc.vector.tensor_scalar(out=var[:], in0=var[:], scalar1=1.0 / (n - 1.0), scalar2=0.0, op0=ALU.mult, op1=ALU.max)
            nc.gpsimd.tensor_tensor(out=stat_std[m][:], in0=var[:], in1=half[:], op=ALU.pow)

        def stats_b(m):
            std = stat_std[m]
            nc.vector.tensor_scalar(out=std[:], in0=std[:], scalar1=EPS, scalar2=None, op0=ALU.add)
            nc.vector.reciprocal(out=rinv[m][:], in_=std[:])
            nc.vector.tensor_tensor(out=nbias[m][:], in0=negmean[m][:], in1=rinv[m][:], op=ALU.mult)

        def norm(m, q, width, on_scalar):
            cols = slice(q * CH, q * CH + width)
            for r in range(RT):
                if r in on_scalar:
                    nc.scalar.activation(
                        out=va[m][:, r, cols], in_=va[m][:, r, cols], func=ACT.Identity,
                        scale=rinv[m][:, r:r + 1], bias=nbias[m][:, r:r + 1],
                    )
                else:
                    nc.vector.tensor_scalar(
                        out=va[m][:, r, cols], in0=va[m][:, r, cols],
                        scalar1=negmean[m][:, r:r + 1], scalar2=rinv[m][:, r:r + 1],
                        op0=ALU.add, op1=ALU.mult,
                    )

        def fa(q, on_vector=()):
            for jt in range(4 * q, 4 * q + 4):
                cols = slice(jt * P, (jt + 1) * P)
                pf = psum.tile([P, RT, P], F32, tag="tp", name="pf")
                for r in range(RT):
                    nc.tensor.transpose(pf[:, r, :], va[0][:, r, cols], ident_f[:])
                if jt % 4 in on_vector:
                    nc.vector.tensor_scalar(
                        out=va[0][:, :, cols], in0=pf[:], scalar1=vcf[:, jt:jt + 1], scalar2=lbc[:, jt:jt + 1],
                        op0=ALU.mult, op1=ALU.add,
                    )
                else:
                    nc.scalar.activation(
                        out=va[0][:, :, cols], in_=pf[:], func=ACT.Identity,
                        scale=vcf[:, jt:jt + 1], bias=lbc[:, jt:jt + 1],
                    )

        def fb(q):
            for jt in range(4 * q, 4 * q + 4):
                cols = slice(jt * P, (jt + 1) * P)
                pf = psum.tile([P, RT, P], F32, tag="tp", name="pf")
                for r in range(RT):
                    nc.tensor.transpose(pf[:, r, :], va[1][:, r, cols], ident_f[:])
                nc.vector.scalar_tensor_tensor(
                    out=va[0][:, :, cols], in0=pf[:], scalar=vcf[:, 32 + jt:33 + jt], in1=va[0][:, :, cols],
                    op0=ALU.mult, op1=ALU.add,
                )

        def bphase(q):
            gate = q // 2
            cols = slice(q * CH, (q + 1) * CH)
            for r in range(RT):
                pb = psum.tile([P, CH], F32, tag="acc", name="pb")
                for t in range(4):
                    jt = 4 * q + t
                    nc.tensor.transpose(pb[:, t * P:(t + 1) * P], va[0][:, r, jt * P:(jt + 1) * P], ident_f[:])
                if gate == 1:
                    nc.scalar.activation(out=va[1][:, r, cols], in_=pb[:], func=ACT.Sigmoid, bias=negone[:, 0:1], scale=1.0)
                elif gate == 3:
                    nc.scalar.activation(out=va[1][:, r, cols], in_=pb[:], func=ACT.Tanh)
                else:
                    nc.scalar.activation(out=va[1][:, r, cols], in_=pb[:], func=ACT.Sigmoid)

        first = prep_load(acts[0], pieces=4)
        loaded, nxt = load_w(0)
        for part, codes, scales in ((first, acodes[0], ascales[0]), (loaded, nxt[0], nxt[1])):
            for g in range(2):
                prep_half(part, codes, scales, g, vector_copies=((0, 1), (1, 1)))
        for idx in range(2 * NCH):
            cur = nxt
            if idx == NCH - 2:
                prep(acts[1], acodes[1], ascales[1])
            if idx == NCH + 2:
                nc.sync.dma_start(out=cx_sb[:], in_=cx.rearrange("(r p) h -> p r h", p=P))
            more = idx + 1 < 2 * NCH
            if more:
                loaded, nxt = load_w(idx + 1)
                prep_half(loaded, nxt[0], nxt[1], 0)
            mx_rows(idx, cur, (0, 1))
            if more:
                prep_half(loaded, nxt[0], nxt[1], 1)
            mx_rows(idx, cur, (2, 3))
            squares(idx)
            if idx == NCH:
                stats_a(0)
            if idx == NCH + 1:
                stats_b(0)
            if idx == 1:
                nc.sync.dma_start(out=vr3[0:8, :], in_=ln_h2o_w.rearrange("o (t j) -> (o t) j", j=P))
                nc.sync.dma_start(out=vr3[8:16, :], in_=ln_h2o_b.rearrange("o (t j) -> (o t) j", j=P))
            if idx == 3:
                vecs()
            if idx in (NCH + 2, NCH + 4):
                norm(0, (2, 0)[(idx - NCH - 2) // 2], H, (3,))
        fa(2, on_vector=(1, 3))
        fa(0, on_vector=(1, 3))
        stats_a(1)
        norm(0, 6, H, (3,))
        fa(6)
        fa(3)
        stats_b(1)

        s3 = const.tile([P, RT], F32, name="s3")
        negm3 = const.tile([P, RT], F32, name="negm3")
        r3 = const.tile([P, RT], F32, name="r3")

        def parts(r):
            return (va[1][:, r, 0:H], va[1][:, r, H:2 * H], va[1][:, r, 2 * H:3 * H], va[1][:, r, 3 * H:4 * H],
                    va[0][:, r, 0:H], va[0][:, r, H:2 * H], va[0][:, r, 3 * H:4 * H], va[0][:, r, 2 * H:3 * H])

        s3h = const.tile([P, RT, 2], F32, name="s3h")

        def cab(hf, rows):
            cc = slice(hf * CH, (hf + 1) * CH)
            for r in rows:
                gi, gf, go, gc, t0, t1, cn, hn = parts(r)
                nc.vector.tensor_tensor(out=t0[:, cc], in0=gf[:, cc], in1=cx_sb[:, r, cc], op=ALU.mult)
                nc.vector.tensor_tensor(out=t1[:, cc], in0=gi[:, cc], in1=gc[:, cc], op=ALU.mult)
            for r in rows:
                gi, gf, go, gc, t0, t1, cn, hn = parts(r)
                nc.vector.scalar_tensor_tensor(
                    out=cn[:, cc], in0=t0[:, cc], scalar=1.0, in1=t1[:, cc], op0=ALU.mult, op1=ALU.add,
                    accum_out=s3h[:, r, hf:hf + 1],
                )

        sh3 = const.tile([P, RT], F32, name="sh3")
        q3h = const.tile([P, RT, 2], F32, name="q3h")

        def squares3(hf, rows):
            for r in rows:
                gi, gf, go, gc, t0, t1, cn, hn = parts(r)
                junk = stage.tile([P, CH], BF16, tag="junk", name="junk")
                nc.scalar.activation(
                    out=junk[:], in_=cn[:, hf * CH:(hf + 1) * CH], func=ACT.Square,
                    bias=sh3[:, r:r + 1], scale=1.0, accum_out=q3h[:, r, hf:hf + 1],
                )

        def ln3_stats(h):
            rr = slice(2 * h, 2 * h + 2)
            for r in (2 * h, 2 * h + 1):
                nc.sync.dma_start(out=out_1[r * P:(r + 1) * P, :], in_=parts(r)[6])
            nc.vector.tensor_tensor(out=s3[:, rr], in0=s3h[:, rr, 0], in1=s3h[:, rr, 1], op=ALU.add)
            nc.vector.tensor_scalar(out=negm3[:, rr], in0=s3[:, rr], scalar1=-1.0 / H, scalar2=None, op0=ALU.mult)
            nc.vector.tensor_tensor(out=d3[h][:], in0=sh3[:, rr], in1=negm3[:, rr], op=ALU.subtract)
            nc.vector.scalar_tensor_tensor(out=d3[h][:], in0=d3[h][:], scalar=float(H), in1=d3[h][:], op0=ALU.mult, op1=ALU.mult)
            nc.vector.tensor_tensor(out=d3[h][:], in0=q3h[:, rr, 0], in1=d3[h][:], op=ALU.subtract)
            squares3(1, (2 * h, 2 * h + 1))
            nc.vector.tensor_tensor(out=var3[h][:], in0=q3h[:, rr, 1], in1=d3[h][:], op=ALU.add)
            nc.vector.tensor_scalar(
                out=var3[h][:], in0=var3[h][:], scalar1=1.0 / (H - 1.0), scalar2=0.0, op0=ALU.mult, op1=ALU.max,
            )
            nc.gpsimd.tensor_tensor(out=std3[h][:], in0=var3[h][:], in1=half[:, 0:2], op=ALU.pow)

        d3 = [const.tile([P, 2], F32, name="d3_%d" % h) for h in range(2)]
        var3 = [const.tile([P, 2], F32, name="var3_%d" % h) for h in range(2)]
        std3 = [const.tile([P, 2], F32, name="std3_%d" % h) for h in range(2)]

        def ln3_norm(h):
            rr = slice(2 * h, 2 * h + 2)
            nc.vector.tensor_scalar(out=std3[h][:], in0=std3[h][:], scalar1=EPS, scalar2=None, op0=ALU.add)
            nc.vector.reciprocal(out=r3[:, rr], in_=std3[h][:])
            for r in (2 * h, 2 * h + 1):
                gi, gf, go, gc, t0, t1, cn, hn = parts(r)
                nc.vector.tensor_scalar(
                    out=t1, in0=cn, scalar1=negm3[:, r:r + 1], scalar2=r3[:, r:r + 1], op0=ALU.add, op1=ALU.mult,
                )

        def ln3_tanh(h):
            for t in range(0, H // P, 2):
                pf = psum.tile([P, 2, 2, P], F32, tag="tp", name="pf")
                for i in range(2):
                    for k in range(2):
                        nc.tensor.transpose(
                            pf[:, i, k, :], va[0][:, 2 * h + k, H + (t + i) * P:H + (t + i + 1) * P], ident_f[:],
                        )
                for i in range(2):
                    nc.scalar.activation(
                        out=va[0][:, 2 * h:2 * h + 2, (t + i) * P:(t + i + 1) * P], in_=pf[:, i, :, :], func=ACT.Tanh,
                        scale=vcf3[:, t + i:t + i + 1], bias=vcf3[:, 8 + t + i:9 + t + i],
                    )

        def fin(h):
            for r in (2 * h, 2 * h + 1):
                gi, gf, go, gc, t0, t1, cn, hn = parts(r)
                for c in range(2):
                    cc = slice(c * CH, (c + 1) * CH)
                    pb = psum.tile([P, CH], F32, tag="acc", name="pb")
                    for t in range(4):
                        nc.tensor.transpose(pb[:, t * P:(t + 1) * P], t0[:, c * CH + t * P:c * CH + (t + 1) * P], ident_f[:])
                    nc.vector.tensor_tensor(out=hn[:, cc], in0=go[:, cc], in1=pb[:], op=ALU.mult)
                nc.sync.dma_start(out=out_0[r * P:(r + 1) * P, :], in_=hn)

        norm(1, 2, CH, ())
        norm(1, 0, CH, (3,))
        fb(2)
        norm(1, 6, H, (3,))
        fb(0)
        bphase(2)
        norm(1, 3, CH, (3,))
        fb(6)
        bphase(0)
        fa(1)
        fb(3)
        bphase(6)
        norm(1, 1, CH, (3,))
        cab(0, (0, 1))
        fb(1)
        bphase(3)
        fa(7)
        cab(0, (2, 3))
        fb(7)
        bphase(1)
        nc.vector.tensor_scalar(out=sh3[:], in0=s3h[:, :, 0], scalar1=-1.0 / CH, scalar2=None, op0=ALU.mult)
        norm(0, 4, H, (3,))
        norm(1, 4, H, (3,))
        fa(4)
        bphase(7)
        squares3(0, range(RT))
        cab(1, (0, 1))
        ln3_stats(0)
        fb(4)
        fa(5)
        cab(1, (2, 3))
        ln3_stats(1)
        bphase(4)
        fb(5)
        ln3_norm(0)
        ln3_tanh(0)
        bphase(5)
        ln3_norm(1)
        ln3_tanh(1)
        for h in range(2):
            fin(h)
